import numpy as np
import ml_dtypes


def mxq(x, axis, fmt="e4m3"):
    dtype, down = {"e4m3": (ml_dtypes.float8_e4m3fn, 7), "e5m2": (ml_dtypes.float8_e5m2, 14)}[fmt]
    v = np.moveaxis(np.asarray(x, np.float32).astype(ml_dtypes.bfloat16).astype(np.float64), axis, -1)
    blocks = v.reshape(v.shape[:-1] + (-1, 32))
    amax = np.abs(blocks).max(-1, keepdims=True)
    byte = np.maximum(np.where(amax > 0, np.frexp(amax)[1] - 1 + 127, 0) - down, 1)
    scale = np.exp2(byte - 127.0)
    codes = (blocks / scale).astype(np.float32).astype(dtype).astype(np.float64)
    return np.moveaxis((codes * scale).reshape(v.shape), -1, axis)


WIDE = False


def mx_kscale(k):
    if not WIDE:
        return np.ones(k)
    levels = np.array([10, -10, 5, -5, 0])
    if k % 512:
        return np.exp2(np.random.permutation(np.resize(levels, k // 32))).repeat(32)
    a = np.empty((k // 512, 16))
    for p in range(k // 512):
        a[p, :8] = np.random.permutation(np.resize(levels, 8))
        for g in range(8):
            far = levels[np.abs(levels - a[p, g]) >= 10]
            a[p, g + 8] = far[np.random.randint(len(far))]
    return np.exp2(a.ravel()).repeat(32)


BF16 = ml_dtypes.bfloat16


def bf(x):
    return np.asarray(x, np.float32).astype(BF16)


def f64(x):
    return np.asarray(x).astype(np.float64)


B, S, D, QL, KL, H = 2, 2048, 512, 512, 512, 4
HD = D // H
ROPE_BASE = 10000.0


def rope(x):
    d = x.shape[-1]
    half = d // 2
    inv_freq = 1.0 / (ROPE_BASE ** (np.arange(half, dtype=np.float64) * 2.0 / d))
    pos = np.arange(x.shape[1], dtype=np.float64)
    ang = pos[:, None] * inv_freq[None, :]
    cos = np.concatenate([np.cos(ang), np.cos(ang)], -1)[None]
    sin = np.concatenate([np.sin(ang), np.sin(ang)], -1)[None]
    x1, x2 = x[..., :half], x[..., half:]
    rot = np.concatenate([-x2, x1], -1)
    return x * cos + rot * sin


def draw0():
    s, t = mx_kscale(D), mx_kscale(QL)
    return {"inputs_q": bf(np.random.standard_normal((B, S, D)) * s),
            "Wq_down": bf(np.random.standard_normal((D, QL)) / np.sqrt(D) / s[:, None] * t),
            "Wq_up": bf(np.random.standard_normal((QL, D)) / np.sqrt(QL) / t[:, None]),
            "Wq_rope": bf(np.random.standard_normal((QL, D)) / np.sqrt(QL) / t[:, None])}


def core(inputs_q, Wq_down, Wq_up, Wq_rope):
    q_latent = mxq(f64(inputs_q), 2, "e4m3") @ mxq(f64(Wq_down), 0, "e4m3")
    lq = mxq(q_latent, 2, "e4m3")
    q_proj = (lq @ mxq(f64(Wq_up), 0, "e4m3")).reshape(B, S, H, HD)
    q_rope = rope(lq @ mxq(f64(Wq_rope), 0, "e4m3")).reshape(B, S, H, HD)
    return np.concatenate([q_proj, q_rope], -1)


def e4m3fn_bytes(y):
    return np.clip(np.asarray(y, np.float64), -448.0, 448.0).astype(np.float32).astype(ml_dtypes.float8_e4m3fn).view(np.uint8)


def e4m3fn_values(b):
    return np.asarray(b, np.uint8).view(ml_dtypes.float8_e4m3fn).astype(np.float64)


def setup_inputs():
    d = draw0()
    x0 = np.asarray(d['inputs_q']).astype(np.float64)
    s = (np.max(np.abs(x0), axis=(0, 1), keepdims=True) / 448.0).astype(np.float32)
    out = {}
    for k, v in d.items():
        if k == 'inputs_q':
            out['inputs_q_bytes'] = e4m3fn_bytes(x0 / s.astype(np.float64))
            out['inputs_q_scale'] = s
        else:
            out[k] = v
    return out


def reference(inputs_q_bytes, inputs_q_scale, Wq_down, Wq_up, Wq_rope):
    return core(e4m3fn_values(inputs_q_bytes) * inputs_q_scale.astype(np.float64), Wq_down, Wq_up, Wq_rope)

@@ -1,0 +1,254 @@
+import math
+from contextlib import ExitStack
+
+import concourse.mybir as mybir
+from concourse.masks import make_identity
+
+B, S, D, QL = 2, 2048, 512, 512
+HALF = 256
+P = 128
+PACK = 4
+NI = S // P
+FLOPS = 2 * B * S * D * 3 * QL
+
+F32 = mybir.dt.float32
+BF16 = mybir.dt.bfloat16
+I32 = mybir.dt.int32
+U32 = mybir.dt.uint32
+U8 = mybir.dt.uint8
+FP8 = mybir.dt.float8_e4m3fn
+FP8X4 = mybir.dt.float8_e4m3fn_x4
+ALU = mybir.AluOpType
+ACT = mybir.ActivationFunctionType
+
+X_CHUNKS = ((0, 2), (2, 4), (4, 8), (8, 16))
+
+
+def tile_multiheadlatentattention_pa_t_kernel(tc, x_bytes, x_scale, wq_down, wq_up, wq_rope, out):
+    nc = tc.nc
+    with ExitStack() as ctx:
+        keep = ctx.enter_context(tc.tile_pool(name="keep", bufs=1))
+        work = ctx.enter_context(tc.tile_pool(name="work", bufs=2))
+        work3 = ctx.enter_context(tc.tile_pool(name="work3", bufs=3))
+        outs = ctx.enter_context(tc.tile_pool(name="outs", bufs=3))
+        ps1 = ctx.enter_context(tc.psum_pool(name="ps1", bufs=1))
+        ctx.enter_context(tc.manual_schedule())
+
+        sc4 = keep.tile([P, PACK], F32, name="sc4")
+        nc.sync.dma_start(out=sc4[:], in_=x_scale.rearrange("a b (p t) -> p (a b t)", t=PACK))
+        x_view = x_bytes.rearrange("b (p i) k -> p i b k", i=NI)
+        x_tiles = {}
+
+        def load_x(lo, hi):
+            t = keep.tile([P, hi - lo, B, D], U8, name="xb%d" % lo)
+            for b in range(B):
+                nc.sync.dma_start(out=t[:, :, b, :], in_=x_view[:, lo:hi, b, :])
+            for i in range(lo, hi):
+                x_tiles[i] = t[:, i - lo, :, :]
+
+        def load_w(w, name):
+            t = keep.tile([P, PACK, 512], BF16, name=name)
+            nc.sync.dma_start(out=t[:], in_=w.rearrange("(p j) c -> p j c", j=PACK))
+            return t
+
+        load_x(0, 2)
+        wd_raw = load_w(wq_down, "wd_raw")
+        load_x(2, 4)
+        wr_raw = load_w(wq_rope, "wr_raw")
+        wu_raw = load_w(wq_up, "wu_raw")
+        load_x(4, 8)
+        load_x(8, 16)
+
+        ones = keep.tile([P, 1], F32, name="ones")
+        nc.vector.memset(ones[:], 1.0)
+        dummy = keep.tile([P, 1], F32, name="dummy")
+        nc.scalar.activation(dummy[:], ones[:], ACT.Sin)
+        ident = keep.tile([P, P], F32, name="ident")
+        make_identity(nc, ident[:])
+        pos = keep.tile([P, NI], F32, name="pos")
+        nc.gpsimd.iota(pos[:], pattern=[[1, NI]], base=0, channel_multiplier=NI, allow_small_or_imprecise_dtypes=True)
+        freq = keep.tile([P, HALF], F32, name="freq")
+        nc.vector.tensor_scalar(freq[:, 0:1], ones[:], 1.0 / (2.0 * math.pi), None, op0=ALU.mult)
+        width = 1
+        while width < HALF:
+            nc.vector.tensor_scalar(freq[:, width : 2 * width], freq[:, 0:width], 10000.0 ** (-width / 256.0), None, op0=ALU.mult)
+            width *= 2
+
+        turns = keep.tile([P, NI, HALF], I32, name="turns")
+
+        def count_turns(i):
+            nc.gpsimd.tensor_scalar(turns[:, i, :], freq[:], pos[:, i : i + 1], -0.125, op0=ALU.mult, op1=ALU.add)
+
+        wd_c = keep.tile([P, 512], U32, name="wd_c", align_bytes=64)
+        wd_s = keep.tile([P, 512], U8, name="wd_s", align_bytes=64)
+        wr_c = keep.tile([P, 512], U32, name="wr_c", align_bytes=64)
+        wr_s = keep.tile([P, 512], U8, name="wr_s", align_bytes=64)
+        wu_c = keep.tile([P, 512], U32, name="wu_c", align_bytes=64)
+        wu_s = keep.tile([P, 512], U8, name="wu_s", align_bytes=64)
+        wd_g = keep.tile([P, 512, PACK], BF16, name="wd_g", align_bytes=64)
+        wr_g = keep.tile([P, 512, PACK], BF16, name="wr_g", align_bytes=64)
+        wu_g = keep.tile([P, 512, PACK], BF16, name="wu_g", align_bytes=64)
+
+        def quant(codes, scales, src):
+            nc.vector.quantize_mx(out=codes.bitcast(FP8X4), scales=scales, in_=src)
+
+        def mm(o, lc, ls, rc, rs_, start=True, stop=True):
+            nc.tensor.matmul_mx(out=o, lhsT=lc.bitcast(FP8X4), lhsT_scale=ls, rhs=rc.bitcast(FP8X4), rhs_scale=rs_, start=start, stop=stop)
+
+        widened, xt, xg, xq, lq, lb, lqq, rr, rs, qp, frac, ab, csum, t2, k1, ot = ({} for _ in range(16))
+
+        def widen(i):
+            widened[i] = work3.tile([P, B * D], BF16, name="widened")
+            nc.scalar.copy(widened[i][:], x_tiles[i].rearrange("p b k -> p (b k)").bitcast(FP8))
+
+        def transpose_x(i):
+            xt[i] = ps1.tile([P, 2, 256], F32, name="xt")
+            words = widened[i][:].bitcast(F32)
+            for b in range(B):
+                for u in range(2):
+                    nc.tensor.transpose(xt[i][:, u, 128 * b : 128 * b + 128], words[:, 256 * b + u : 256 * (b + 1) : 2], ident[:])
+
+        def scale_x(i):
+            xg[i] = work.tile([P, 256, PACK], BF16, name="xg", align_bytes=64)
+            nc.vector.tensor_tensor(
+                out=xg[i][:].rearrange("p r (u e) -> p r u e", u=2),
+                in0=xt[i][:].rearrange("p u r -> p (u r)").bitcast(BF16).rearrange("p (u r e) -> p r u e", u=2, e=2),
+                in1=sc4[:].rearrange("p (u e) -> p u e", u=2).unsqueeze(1).to_broadcast([P, 256, 2, 2]),
+                op=ALU.mult,
+            )
+
+        def quant_x(i):
+            c = work3.tile([P, 256], U32, name="xq_c", align_bytes=64)
+            s = work3.tile([P, 256], U8, name="xq_s", align_bytes=64)
+            quant(c[:], s[:], xg[i][:].rearrange("p r j -> p (r j)"))
+            xq[i] = (c, s)
+
+        def stage1(i):
+            c, s = xq[i]
+            lq[i] = [ps1.tile([P, PACK, 128], F32, name="lq0"), ps1.tile([P, PACK, 128], F32, name="lq1")]
+            for b in range(B):
+                cols = slice(128 * b, 128 * b + 128)
+                for t in range(PACK):
+                    wcols = slice(128 * t, 128 * t + 128)
+                    mm(lq[i][b][:, t, :], wd_c[:, wcols], wd_s[:, wcols], c[:, cols], s[:, cols])
+
+        def copy_lq(i):
+            lb[i] = work.tile([P, B, 128, PACK], BF16, name="lb", align_bytes=64)
+            for b in range(B):
+                nc.scalar.copy(lb[i][:, b, :, :], lq[i][b][:].rearrange("p t r -> p r t"))
+
+        def quant_lq(i):
+            c = work3.tile([P, 256], U32, name="lq_c", align_bytes=64)
+            s = work3.tile([P, 256], U8, name="lq_s", align_bytes=64)
+            quant(c[:], s[:], lb[i][:].rearrange("p b r j -> p (b r j)"))
+            lqq[i] = (c, s)
+
+        def rope_mm(i):
+            c, s = lqq[i]
+            rr[i] = [ps1.tile([P, 512], F32, name="rr0"), ps1.tile([P, 512], F32, name="rr1")]
+            rs[i] = ps1.tile([P, B, HALF], F32, name="rs")
+            for b in range(B):
+                cols = slice(128 * b, 128 * b + 128)
+                mm(rr[i][b][:], c[:, cols], s[:, cols], wr_c[:], wr_s[:])
+            for b in range(B):
+                cols = slice(128 * b, 128 * b + 128)
+                mm(rs[i][:, b, :], c[:, cols], s[:, cols], wr_c[:, 0:HALF], wr_s[:, 0:HALF], start=True, stop=False)
+                mm(rs[i][:, b, :], c[:, cols], s[:, cols], wr_c[:, HALF:512], wr_s[:, HALF:512], start=False, stop=True)
+
+        def proj_mm(i):
+            c, s = lqq[i]
+            qp[i] = [ps1.tile([P, 512], F32, name="qp0"), ps1.tile([P, 512], F32, name="qp1")]
+            for b in range(B):
+                cols = slice(128 * b, 128 * b + 128)
+                mm(qp[i][b][:], c[:, cols], s[:, cols], wu_c[:], wu_s[:])
+
+        def angle_frac(i):
+            frac[i] = work3.tile([P, HALF], F32, name="frac")
+            nc.vector.scalar_tensor_tensor(frac[i][:], freq[:], pos[:, i : i + 1], turns[:, i, :], op0=ALU.mult, op1=ALU.subtract)
+
+        def sines(i):
+            ab[i] = work3.tile([P, 2, HALF], F32, name="ab")
+            mag = work.tile([P, HALF], F32, name="mag")
+            nc.scalar.activation(ab[i][:, 1, :], frac[i][:], ACT.Sin, bias=math.pi / 4, scale=-2 * math.pi)
+            nc.scalar.activation(mag[:], frac[i][:], ACT.Abs, bias=-0.125, scale=1.0)
+            nc.scalar.activation(ab[i][:, 0, :], mag[:], ACT.Sin, bias=math.pi / 2, scale=-2 * math.pi)
+
+        def sum_ab(i):
+            csum[i] = work.tile([P, HALF], F32, name="csum")
+            nc.vector.tensor_tensor(out=csum[i][:], in0=ab[i][:, 0, :], in1=ab[i][:, 1, :], op=ALU.add)
+
+        def rope_products(i):
+            t2[i] = work.tile([P, B, 512], F32, name="t2")
+            for b in range(B):
+                nc.vector.scalar_tensor_tensor(t2[i][:, b, :], rr[i][b][:], math.sqrt(2.0), ab[i][:].rearrange("p f c -> p (f c)"), op0=ALU.mult, op1=ALU.mult)
+
+        def rope_common(i):
+            k1[i] = work.tile([P, B, HALF], F32, name="k1")
+            for b in range(B):
+                nc.vector.scalar_tensor_tensor(k1[i][:, b, :], rs[i][:, b, :], math.sqrt(0.5), csum[i][:], op0=ALU.mult, op1=ALU.mult)
+
+        def copy_proj(i):
+            ot[i] = [outs.tile([P, 4, 256], F32, name="ot0"), outs.tile([P, 4, 256], F32, name="ot1")]
+            for b in range(B):
+                nc.scalar.copy(ot[i][b][:, :, 0:128], qp[i][b][:].rearrange("p (h c) -> p h c", h=4))
+
+        out_view = out.rearrange("b (p i) h c -> b i p h c", i=NI)
+
+        def rope_sum_and_store(i):
+            for b in range(B):
+                for f in range(2):
+                    nc.gpsimd.tensor_tensor(
+                        out=ot[i][b][:, 2 * f : 2 * f + 2, 128:256],
+                        in0=k1[i][:, b, :].rearrange("p (h c) -> p h c", h=2),
+                        in1=t2[i][:, b, 256 * f : 256 * f + 256].rearrange("p (h c) -> p h c", h=2),
+                        op=ALU.subtract,
+                    )
+                nc.sync.dma_start(out=out_view[b, i], in_=ot[i][b][:])
+
+        def at(i, stage):
+            if 0 <= i < NI:
+                stage(i)
+
+        for i in range(3):
+            count_turns(i)
+        angle_frac(0)
+        for f in range(2):
+            nc.gpsimd.tensor_scalar(
+                wr_g[:, 256 * f : 256 * f + 256, :],
+                wr_raw[:, :, 256 - 256 * f : 512 - 256 * f].rearrange("p j c -> p c j"),
+                1.0, 0.0, op0=ALU.mult, op1=ALU.add,
+            )
+        nc.gpsimd.tensor_scalar(wu_g[:], wu_raw[:].rearrange("p j c -> p c j"), 1.0, 0.0, op0=ALU.mult, op1=ALU.add)
+        for i in range(3, NI):
+            count_turns(i)
+
+        widen(0)
+        transpose_x(0)
+        widen(1)
+        nc.vector.tensor_copy(
+            out=wd_g[:].rearrange("p (t m) j -> p t m j", t=PACK),
+            in_=wd_raw[:].rearrange("p j (m t) -> p t m j", t=PACK),
+        )
+        for k in range(-2, NI + 1):
+            at(k, rope_mm)
+            at(k + 2, scale_x)
+            if k == -2:
+                quant(wd_c[:], wd_s[:], wd_g[:].rearrange("p n j -> p (n j)"))
+            at(k + 1, stage1)
+            at(k + 4, widen)
+            at(k + 2, sines)
+            at(k, rope_products)
+            if k == 0:
+                quant(wu_c[:], wu_s[:], wu_g[:].rearrange("p n j -> p (n j)"))
+            at(k + 1, copy_lq)
+            at(k, proj_mm)
+            at(k - 1, rope_sum_and_store)
+            at(k, copy_proj)
+            at(k + 3, transpose_x)
+            at(k + 2, quant_x)
+            at(k + 3, angle_frac)
+            at(k + 1, sum_ab)
+            at(k + 1, quant_lq)
+            if k == -1:
+                quant(wr_c[:], wr_s[:], wr_g[:].rearrange("p n j -> p (n j)"))
+            at(k, rope_common)

@@ -8,6 +8,7 @@ B, S, D, QL = 2, 2048, 512, 512
 HALF = 256
 P = 128
 PACK = 4
+WRAP = 176
 NI = S // P
 FLOPS = 2 * B * S * D * 3 * QL
 
@@ -20,8 +21,6 @@ FP8 = mybir.dt.float8_e4m3fn
 FP8X4 = mybir.dt.float8_e4m3fn_x4
 ALU = mybir.AluOpType
 ACT = mybir.ActivationFunctionType
-
-X_CHUNKS = ((0, 2), (2, 4), (4, 8), (8, 16))
 
 
 def tile_multiheadlatentattention_pa_t_kernel(tc, x_bytes, x_scale, wq_down, wq_up, wq_rope, out):
@@ -51,13 +50,13 @@ def tile_multiheadlatentattention_pa_t_kernel(tc, x_bytes, x_scale, wq_down, wq_
             nc.sync.dma_start(out=t[:], in_=w.rearrange("(p j) c -> p j c", j=PACK))
             return t
 
-        load_x(0, 2)
+        load_x(0, 1)
         wd_raw = load_w(wq_down, "wd_raw")
-        load_x(2, 4)
+        load_x(1, 4)
         wr_raw = load_w(wq_rope, "wr_raw")
         wu_raw = load_w(wq_up, "wu_raw")
-        load_x(4, 8)
-        load_x(8, 16)
+        load_x(4, 10)
+        load_x(10, 16)
 
         ones = keep.tile([P, 1], F32, name="ones")
         nc.vector.memset(ones[:], 1.0)
@@ -73,11 +72,13 @@ def tile_multiheadlatentattention_pa_t_kernel(tc, x_bytes, x_scale, wq_down, wq_
         while width < HALF:
             nc.vector.tensor_scalar(freq[:, width : 2 * width], freq[:, 0:width], 10000.0 ** (-width / 256.0), None, op0=ALU.mult)
             width *= 2
+        slope = keep.tile([P, NI], F32, name="slope")
+        nc.vector.tensor_scalar(slope[:], pos[:], -2 * math.pi, None, op0=ALU.mult)
 
-        turns = keep.tile([P, NI, HALF], I32, name="turns")
+        turns = keep.tile([P, NI, WRAP], I32, name="turns")
 
         def count_turns(i):
-            nc.gpsimd.tensor_scalar(turns[:, i, :], freq[:], pos[:, i : i + 1], -0.125, op0=ALU.mult, op1=ALU.add)
+            nc.gpsimd.tensor_scalar(turns[:, i, :], freq[:, 0:WRAP], pos[:, i : i + 1], -0.125, op0=ALU.mult, op1=ALU.add)
 
         wd_c = keep.tile([P, 512], U32, name="wd_c", align_bytes=64)
         wd_s = keep.tile([P, 512], U8, name="wd_s", align_bytes=64)
@@ -99,7 +100,11 @@ def tile_multiheadlatentattention_pa_t_kernel(tc, x_bytes, x_scale, wq_down, wq_
 
         def widen(i):
             widened[i] = work3.tile([P, B * D], BF16, name="widened")
-            nc.scalar.copy(widened[i][:], x_tiles[i].rearrange("p b k -> p (b k)").bitcast(FP8))
+            if i == 0:
+                nc.scalar.copy(widened[i][:, 0:D], x_tiles[i][:, 0, :].bitcast(FP8))
+                nc.vector.tensor_copy(out=widened[i][:, D : 2 * D], in_=x_tiles[i][:, 1, :].bitcast(FP8))
+            else:
+                nc.scalar.copy(widened[i][:], x_tiles[i].rearrange("p b k -> p (b k)").bitcast(FP8))
 
         def transpose_x(i):
             xt[i] = ps1.tile([P, 2, 256], F32, name="xt")
@@ -163,15 +168,17 @@ def tile_multiheadlatentattention_pa_t_kernel(tc, x_bytes, x_scale, wq_down, wq_
                 mm(qp[i][b][:], c[:, cols], s[:, cols], wu_c[:], wu_s[:])
 
         def angle_frac(i):
-            frac[i] = work3.tile([P, HALF], F32, name="frac")
-            nc.vector.scalar_tensor_tensor(frac[i][:], freq[:], pos[:, i : i + 1], turns[:, i, :], op0=ALU.mult, op1=ALU.subtract)
+            frac[i] = work3.tile([P, WRAP], F32, name="frac")
+            nc.vector.scalar_tensor_tensor(frac[i][:], freq[:, 0:WRAP], pos[:, i : i + 1], turns[:, i, :], op0=ALU.mult, op1=ALU.subtract)
 
         def sines(i):
             ab[i] = work3.tile([P, 2, HALF], F32, name="ab")
-            mag = work.tile([P, HALF], F32, name="mag")
-            nc.scalar.activation(ab[i][:, 1, :], frac[i][:], ACT.Sin, bias=math.pi / 4, scale=-2 * math.pi)
+            mag = work.tile([P, WRAP], F32, name="mag")
             nc.scalar.activation(mag[:], frac[i][:], ACT.Abs, bias=-0.125, scale=1.0)
-            nc.scalar.activation(ab[i][:, 0, :], mag[:], ACT.Sin, bias=math.pi / 2, scale=-2 * math.pi)
+            nc.scalar.activation(ab[i][:, 1, 0:WRAP], frac[i][:], ACT.Sin, bias=math.pi / 4, scale=-2 * math.pi)
+            nc.scalar.activation(ab[i][:, 1, WRAP:HALF], freq[:, WRAP:HALF], ACT.Sin, bias=math.pi / 4, scale=slope[:, i : i + 1])
+            nc.scalar.activation(ab[i][:, 0, WRAP:HALF], freq[:, WRAP:HALF], ACT.Sin, bias=3 * math.pi / 4, scale=slope[:, i : i + 1])
+            nc.scalar.activation(ab[i][:, 0, 0:WRAP], mag[:], ACT.Sin, bias=math.pi / 2, scale=-2 * math.pi)
 
         def sum_ab(i):
             csum[i] = work.tile([P, HALF], F32, name="csum")
@@ -184,8 +191,7 @@ def tile_multiheadlatentattention_pa_t_kernel(tc, x_bytes, x_scale, wq_down, wq_
 
         def rope_common(i):
             k1[i] = work.tile([P, B, HALF], F32, name="k1")
-            for b in range(B):
-                nc.vector.scalar_tensor_tensor(k1[i][:, b, :], rs[i][:, b, :], math.sqrt(0.5), csum[i][:], op0=ALU.mult, op1=ALU.mult)
+            nc.vector.scalar_tensor_tensor(k1[i][:], rs[i][:], math.sqrt(0.5), csum[i][:].unsqueeze(1).to_broadcast([P, B, HALF]), op0=ALU.mult, op1=ALU.mult)
 
         def copy_proj(i):
             ot[i] = [outs.tile([P, 4, 256], F32, name="ot0"), outs.tile([P, 4, 256], F32, name="ot1")]
@@ -195,14 +201,17 @@ def tile_multiheadlatentattention_pa_t_kernel(tc, x_bytes, x_scale, wq_down, wq_
         out_view = out.rearrange("b (p i) h c -> b i p h c", i=NI)
 
         def rope_sum_and_store(i):
+            if i < NI - 1:
+                gate = work.tile([P, 1], U8, name="gate")
+                nc.gpsimd.tensor_copy(out=gate[:], in_=lqq[i + 1][1][:, 0:1])
+            engine = nc.gpsimd if i < NI - 1 else nc.vector
             for b in range(B):
-                for f in range(2):
-                    nc.gpsimd.tensor_tensor(
-                        out=ot[i][b][:, 2 * f : 2 * f + 2, 128:256],
-                        in0=k1[i][:, b, :].rearrange("p (h c) -> p h c", h=2),
-                        in1=t2[i][:, b, 256 * f : 256 * f + 256].rearrange("p (h c) -> p h c", h=2),
-                        op=ALU.subtract,
-                    )
+                engine.tensor_tensor(
+                    out=ot[i][b][:].rearrange("p (f h) c -> p f h c", f=2)[:, :, :, 128:256],
+                    in0=k1[i][:, b, :].rearrange("p (h c) -> p h c", h=2).unsqueeze(1).to_broadcast([P, 2, 2, 128]),
+                    in1=t2[i][:, b, :].rearrange("p (f h c) -> p f h c", f=2, h=2),
+                    op=ALU.subtract,
+                )
                 nc.sync.dma_start(out=out_view[b, i], in_=ot[i][b][:])
 
         def at(i, stage):
@@ -211,33 +220,54 @@ def tile_multiheadlatentattention_pa_t_kernel(tc, x_bytes, x_scale, wq_down, wq_
 
         for i in range(3):
             count_turns(i)
-        angle_frac(0)
-        for f in range(2):
-            nc.gpsimd.tensor_scalar(
-                wr_g[:, 256 * f : 256 * f + 256, :],
-                wr_raw[:, :, 256 - 256 * f : 512 - 256 * f].rearrange("p j c -> p c j"),
-                1.0, 0.0, op0=ALU.mult, op1=ALU.add,
-            )
-        nc.gpsimd.tensor_scalar(wu_g[:], wu_raw[:].rearrange("p j c -> p c j"), 1.0, 0.0, op0=ALU.mult, op1=ALU.add)
-        for i in range(3, NI):
-            count_turns(i)
-
+        for i in range(3):
+            angle_frac(i)
         widen(0)
         transpose_x(0)
+        scale_x(0)
+        for t in range(PACK):
+            interleave = nc.vector.tensor_copy if t % 2 else nc.scalar.copy
+            interleave(
+                out=wd_g[:, 128 * t : 128 * t + 128, :],
+                in_=wd_raw[:, :, t : 512 : 4].rearrange("p j m -> p m j"),
+            )
         widen(1)
-        nc.vector.tensor_copy(
-            out=wd_g[:].rearrange("p (t m) j -> p t m j", t=PACK),
-            in_=wd_raw[:].rearrange("p j (m t) -> p t m j", t=PACK),
-        )
-        for k in range(-2, NI + 1):
+        transpose_x(1)
+        sines(0)
+        quant_x(0)
+        quant(wd_c[:], wd_s[:], wd_g[:].rearrange("p n j -> p (n j)"))
+        for q in range(4):
+            nc.gpsimd.tensor_scalar(
+                wu_g[:, 128 * q : 128 * q + 128, :],
+                wu_raw[:, :, 128 * q : 128 * q + 128].rearrange("p j c -> p c j"),
+                1.0, 0.0, op0=ALU.mult, op1=ALU.add,
+            )
+        for i in range(3, NI):
+            count_turns(i)
+        stage1(0)
+        scale_x(1)
+        copy_lq(0)
+        for f in range(2):
+            nc.vector.tensor_copy(
+                out=wr_g[:, 256 * f : 256 * f + 256, :].rearrange("p (c i) j -> p c j i", i=4),
+                in_=wr_raw[:, :, 256 - 256 * f : 512 - 256 * f].rearrange("p j (c i) -> p c j i", i=4),
+            )
+        widen(2)
+        transpose_x(2)
+        widen(3)
+        sines(1)
+        sum_ab(0)
+        quant_x(1)
+        quant_lq(0)
+        quant(wr_c[:], wr_s[:], wr_g[:].rearrange("p n j -> p (n j)"))
+        for k in range(0, NI + 1):
             at(k, rope_mm)
             at(k + 2, scale_x)
-            if k == -2:
-                quant(wd_c[:], wd_s[:], wd_g[:].rearrange("p n j -> p (n j)"))
             at(k + 1, stage1)
             at(k + 4, widen)
             at(k + 2, sines)
             at(k, rope_products)
+            at(k, rope_common)
             if k == 0:
                 quant(wu_c[:], wu_s[:], wu_g[:].rearrange("p n j -> p (n j)"))
             at(k + 1, copy_lq)
@@ -249,6 +279,3 @@ def tile_multiheadlatentattention_pa_t_kernel(tc, x_bytes, x_scale, wq_down, wq_
             at(k + 3, angle_frac)
             at(k + 1, sum_ab)
             at(k + 1, quant_lq)
-            if k == -1:
-                quant(wr_c[:], wr_s[:], wr_g[:].rearrange("p n j -> p (n j)"))
-            at(k, rope_common)

@@ -35,7 +35,7 @@ def tile_multiheadlatentattention_pa_t_kernel(tc, x_bytes, x_scale, wq_down, wq_
 
         sc4 = keep.tile([P, PACK], F32, name="sc4")
         nc.sync.dma_start(out=sc4[:], in_=x_scale.rearrange("a b (p t) -> p (a b t)", t=PACK))
-        x_view = x_bytes.rearrange("b (p i) k -> p i b k", i=NI)
+        x_view = x_bytes.rearrange("b (i p) k -> p i b k", i=NI)
         x_tiles = {}
 
         def load_x(lo, hi):
@@ -58,27 +58,31 @@ def tile_multiheadlatentattention_pa_t_kernel(tc, x_bytes, x_scale, wq_down, wq_
         load_x(4, 10)
         load_x(10, 16)
 
+        pos = keep.tile([P, NI], F32, name="pos")
+        nc.gpsimd.iota(pos[:], pattern=[[P, NI]], base=0, channel_multiplier=1, allow_small_or_imprecise_dtypes=True)
+        ident = keep.tile([P, P], F32, name="ident")
+        make_identity(nc, ident[:])
         ones = keep.tile([P, 1], F32, name="ones")
         nc.vector.memset(ones[:], 1.0)
         dummy = keep.tile([P, 1], F32, name="dummy")
         nc.scalar.activation(dummy[:], ones[:], ACT.Sin)
-        ident = keep.tile([P, P], F32, name="ident")
-        make_identity(nc, ident[:])
-        pos = keep.tile([P, NI], F32, name="pos")
-        nc.gpsimd.iota(pos[:], pattern=[[1, NI]], base=0, channel_multiplier=NI, allow_small_or_imprecise_dtypes=True)
         freq = keep.tile([P, HALF], F32, name="freq")
-        nc.vector.tensor_scalar(freq[:, 0:1], ones[:], 1.0 / (2.0 * math.pi), None, op0=ALU.mult)
-        width = 1
-        while width < HALF:
-            nc.vector.tensor_scalar(freq[:, width : 2 * width], freq[:, 0:width], 10000.0 ** (-width / 256.0), None, op0=ALU.mult)
-            width *= 2
+        for j in range(8):
+            nc.vector.tensor_scalar(freq[:, j : j + 1], ones[:], 10000.0 ** (-j / 256.0) / (2.0 * math.pi), None, op0=ALU.mult)
+        for width in (8, 64):
+            for m in range(1, min(8, HALF // width)):
+                nc.vector.tensor_scalar(freq[:, m * width : (m + 1) * width], freq[:, 0:width], 10000.0 ** (-m * width / 256.0), None, op0=ALU.mult)
         slope = keep.tile([P, NI], F32, name="slope")
         nc.vector.tensor_scalar(slope[:], pos[:], -2 * math.pi, None, op0=ALU.mult)
 
         turns = keep.tile([P, NI, WRAP], I32, name="turns")
+        frac_all = keep.tile([P, NI, WRAP], F32, name="frac_all")
 
         def count_turns(i):
-            nc.gpsimd.tensor_scalar(turns[:, i, :], freq[:, 0:WRAP], pos[:, i : i + 1], -0.125, op0=ALU.mult, op1=ALU.add)
+            nc.vector.tensor_scalar(turns[:, i, :], freq[:, 0:WRAP], pos[:, i : i + 1], -0.125, op0=ALU.mult, op1=ALU.add)
+
+        def angle_frac(i):
+            nc.vector.scalar_tensor_tensor(frac_all[:, i, :], freq[:, 0:WRAP], pos[:, i : i + 1], turns[:, i, :], op0=ALU.mult, op1=ALU.subtract)
 
         wd_c = keep.tile([P, 512], U32, name="wd_c", align_bytes=64)
         wd_s = keep.tile([P, 512], U8, name="wd_s", align_bytes=64)
@@ -96,29 +100,41 @@ def tile_multiheadlatentattention_pa_t_kernel(tc, x_bytes, x_scale, wq_down, wq_
         def mm(o, lc, ls, rc, rs_, start=True, stop=True):
             nc.tensor.matmul_mx(out=o, lhsT=lc.bitcast(FP8X4), lhsT_scale=ls, rhs=rc.bitcast(FP8X4), rhs_scale=rs_, start=start, stop=stop)
 
-        widened, xt, xg, xq, lq, lb, lqq, rr, rs, qp, frac, ab, csum, t2, k1, ot = ({} for _ in range(16))
+        widened, xt, xg, xq, lq, lb, lqq, rr, rs, qp, ab, csum, t2, k1, ot = ({} for _ in range(15))
 
         def widen(i):
             widened[i] = work3.tile([P, B * D], BF16, name="widened")
             if i == 0:
                 nc.scalar.copy(widened[i][:, 0:D], x_tiles[i][:, 0, :].bitcast(FP8))
                 nc.vector.tensor_copy(out=widened[i][:, D : 2 * D], in_=x_tiles[i][:, 1, :].bitcast(FP8))
-            else:
+            elif i < 4:
                 nc.scalar.copy(widened[i][:], x_tiles[i].rearrange("p b k -> p (b k)").bitcast(FP8))
+            else:
+                nc.scalar.copy(widened[i][:, 0:wsplit(i)], x_tiles[i].rearrange("p b k -> p (b k)")[:, 0:wsplit(i)].bitcast(FP8))
 
-        def transpose_x(i):
-            xt[i] = ps1.tile([P, 2, 256], F32, name="xt")
+        def wsplit(i):
+            return 960 if i < 13 else 768
+
+        def widen_v(i):
+            if i >= 4:
+                nc.vector.tensor_copy(out=widened[i][:, wsplit(i) : 1024], in_=x_tiles[i].rearrange("p b k -> p (b k)")[:, wsplit(i) : 1024].bitcast(FP8))
+
+        def transpose_x(i, bs=(0, 1)):
+            if bs[0] == 0:
+                xt[i] = ps1.tile([P, 2, 256], F32, name="xt")
             words = widened[i][:].bitcast(F32)
-            for b in range(B):
+            for b in bs:
                 for u in range(2):
                     nc.tensor.transpose(xt[i][:, u, 128 * b : 128 * b + 128], words[:, 256 * b + u : 256 * (b + 1) : 2], ident[:])
 
-        def scale_x(i):
-            xg[i] = work.tile([P, 256, PACK], BF16, name="xg", align_bytes=64)
+        def scale_x(i, bs=(0, 1)):
+            if bs[0] == 0:
+                xg[i] = work.tile([P, 256, PACK], BF16, name="xg", align_bytes=64)
+            lo, n = 128 * bs[0], 128 * len(bs)
             nc.vector.tensor_tensor(
-                out=xg[i][:].rearrange("p r (u e) -> p r u e", u=2),
-                in0=xt[i][:].rearrange("p u r -> p (u r)").bitcast(BF16).rearrange("p (u r e) -> p r u e", u=2, e=2),
-                in1=sc4[:].rearrange("p (u e) -> p u e", u=2).unsqueeze(1).to_broadcast([P, 256, 2, 2]),
+                out=xg[i][:, lo : lo + n, :].rearrange("p r (u e) -> p r u e", u=2),
+                in0=xt[i][:].rearrange("p u r -> p (u r)").bitcast(BF16).rearrange("p (u r e) -> p r u e", u=2, e=2)[:, lo : lo + n, :, :],
+                in1=sc4[:].rearrange("p (u e) -> p u e", u=2).unsqueeze(1).to_broadcast([P, n, 2, 2]),
                 op=ALU.mult,
             )
 
@@ -167,15 +183,11 @@ def tile_multiheadlatentattention_pa_t_kernel(tc, x_bytes, x_scale, wq_down, wq_
                 cols = slice(128 * b, 128 * b + 128)
                 mm(qp[i][b][:], c[:, cols], s[:, cols], wu_c[:], wu_s[:])
 
-        def angle_frac(i):
-            frac[i] = work3.tile([P, WRAP], F32, name="frac")
-            nc.vector.scalar_tensor_tensor(frac[i][:], freq[:, 0:WRAP], pos[:, i : i + 1], turns[:, i, :], op0=ALU.mult, op1=ALU.subtract)
-
         def sines(i):
             ab[i] = work3.tile([P, 2, HALF], F32, name="ab")
             mag = work.tile([P, WRAP], F32, name="mag")
-            nc.scalar.activation(mag[:], frac[i][:], ACT.Abs, bias=-0.125, scale=1.0)
-            nc.scalar.activation(ab[i][:, 1, 0:WRAP], frac[i][:], ACT.Sin, bias=math.pi / 4, scale=-2 * math.pi)
+            nc.scalar.activation(mag[:], frac_all[:, i, :], ACT.Abs, bias=-0.125, scale=1.0)
+            nc.scalar.activation(ab[i][:, 1, 0:WRAP], frac_all[:, i, :], ACT.Sin, bias=math.pi / 4, scale=-2 * math.pi)
             nc.scalar.activation(ab[i][:, 1, WRAP:HALF], freq[:, WRAP:HALF], ACT.Sin, bias=math.pi / 4, scale=slope[:, i : i + 1])
             nc.scalar.activation(ab[i][:, 0, WRAP:HALF], freq[:, WRAP:HALF], ACT.Sin, bias=3 * math.pi / 4, scale=slope[:, i : i + 1])
             nc.scalar.activation(ab[i][:, 0, 0:WRAP], mag[:], ACT.Sin, bias=math.pi / 2, scale=-2 * math.pi)
@@ -198,33 +210,43 @@ def tile_multiheadlatentattention_pa_t_kernel(tc, x_bytes, x_scale, wq_down, wq_
             for b in range(B):
                 nc.scalar.copy(ot[i][b][:, :, 0:128], qp[i][b][:].rearrange("p (h c) -> p h c", h=4))
 
-        out_view = out.rearrange("b (p i) h c -> b i p h c", i=NI)
+        out_view = out.rearrange("b (i p) h c -> b i p h c", i=NI)
 
         def rope_sum_and_store(i):
             if i < NI - 1:
-                gate = work.tile([P, 1], U8, name="gate")
-                nc.gpsimd.tensor_copy(out=gate[:], in_=lqq[i + 1][1][:, 0:1])
-            engine = nc.gpsimd if i < NI - 1 else nc.vector
+                gate = work.tile([P, 1], F32, name="gate")
+                nc.gpsimd.tensor_copy(out=gate[:], in_=csum[i + 1][:, 0:1])
             for b in range(B):
-                engine.tensor_tensor(
-                    out=ot[i][b][:].rearrange("p (f h) c -> p f h c", f=2)[:, :, :, 128:256],
-                    in0=k1[i][:, b, :].rearrange("p (h c) -> p h c", h=2).unsqueeze(1).to_broadcast([P, 2, 2, 128]),
-                    in1=t2[i][:, b, :].rearrange("p (f h c) -> p f h c", f=2, h=2),
-                    op=ALU.subtract,
-                )
-                nc.sync.dma_start(out=out_view[b, i], in_=ot[i][b][:])
+                last = i == NI - 1 or (i == NI - 2 and b == 1)
+                engine = nc.vector if last else nc.gpsimd
+                for f in range(2) if i == NI - 1 and b == 1 else (slice(0, 2),):
+                    fs = slice(f, f + 1) if isinstance(f, int) else f
+                    n = fs.stop - fs.start
+                    engine.tensor_tensor(
+                        out=ot[i][b][:].rearrange("p (f h) c -> p f h c", f=2)[:, fs, :, 128:256],
+                        in0=k1[i][:, b, :].rearrange("p (h c) -> p h c", h=2).unsqueeze(1).to_broadcast([P, n, 2, 128]),
+                        in1=t2[i][:, b, :].rearrange("p (f h c) -> p f h c", f=2, h=2)[:, fs, :, :],
+                        op=ALU.subtract,
+                    )
+                    nc.sync.dma_start(out=out_view[b, i, :, 2 * fs.start : 2 * fs.stop, :], in_=ot[i][b][:, 2 * fs.start : 2 * fs.stop, :])
 
         def at(i, stage):
             if 0 <= i < NI:
                 stage(i)
 
-        for i in range(3):
+        for i in range(5):
             count_turns(i)
-        for i in range(3):
+        for i in range(5):
             angle_frac(i)
         widen(0)
-        transpose_x(0)
-        scale_x(0)
+        transpose_x(0, (0,))
+        transpose_x(0, (1,))
+        for i in range(5, 8):
+            count_turns(i)
+        for i in range(5, 7):
+            angle_frac(i)
+        scale_x(0, (0,))
+        scale_x(0, (1,))
         for t in range(PACK):
             interleave = nc.vector.tensor_copy if t % 2 else nc.scalar.copy
             interleave(
@@ -236,46 +258,46 @@ def tile_multiheadlatentattention_pa_t_kernel(tc, x_bytes, x_scale, wq_down, wq_
         sines(0)
         quant_x(0)
         quant(wd_c[:], wd_s[:], wd_g[:].rearrange("p n j -> p (n j)"))
-        for q in range(4):
-            nc.gpsimd.tensor_scalar(
-                wu_g[:, 128 * q : 128 * q + 128, :],
-                wu_raw[:, :, 128 * q : 128 * q + 128].rearrange("p j c -> p c j"),
-                1.0, 0.0, op0=ALU.mult, op1=ALU.add,
-            )
-        for i in range(3, NI):
-            count_turns(i)
         stage1(0)
         scale_x(1)
+        widen(2)
+        transpose_x(2)
         copy_lq(0)
         for f in range(2):
             nc.vector.tensor_copy(
                 out=wr_g[:, 256 * f : 256 * f + 256, :].rearrange("p (c i) j -> p c j i", i=4),
                 in_=wr_raw[:, :, 256 - 256 * f : 512 - 256 * f].rearrange("p j (c i) -> p c j i", i=4),
             )
-        widen(2)
-        transpose_x(2)
-        widen(3)
-        sines(1)
-        sum_ab(0)
         quant_x(1)
+        stage1(1)
         quant_lq(0)
         quant(wr_c[:], wr_s[:], wr_g[:].rearrange("p n j -> p (n j)"))
+        sum_ab(0)
+        for f in range(2):
+            (nc.vector.tensor_copy if f else nc.scalar.copy)(
+                out=wu_g[:, 256 * f : 256 * f + 256, :].rearrange("p (c i) j -> p c j i", i=4),
+                in_=wu_raw[:, :, 256 * f : 256 * f + 256].rearrange("p j (c i) -> p c j i", i=4),
+            )
+        widen(3)
+        sines(1)
         for k in range(0, NI + 1):
             at(k, rope_mm)
             at(k + 2, scale_x)
-            at(k + 1, stage1)
-            at(k + 4, widen)
-            at(k + 2, sines)
+            at(k + 1, copy_lq)
             at(k, rope_products)
             at(k, rope_common)
             if k == 0:
                 quant(wu_c[:], wu_s[:], wu_g[:].rearrange("p n j -> p (n j)"))
-            at(k + 1, copy_lq)
             at(k, proj_mm)
-            at(k - 1, rope_sum_and_store)
-            at(k, copy_proj)
             at(k + 3, transpose_x)
+            at(k, copy_proj)
+            at(k - 1, rope_sum_and_store)
+            at(k + 4, widen)
+            at(k + 2, sines)
             at(k + 2, quant_x)
-            at(k + 3, angle_frac)
-            at(k + 1, sum_ab)
+            at(k + 2, stage1)
             at(k + 1, quant_lq)
+            at(k + 7, angle_frac)
+            at(k + 4, widen_v)
+            at(k + 8, count_turns)
+            at(k + 1, sum_ab)

@@ -8,7 +8,13 @@ B, S, D, QL = 2, 2048, 512, 512
 HALF = 256
 P = 128
 PACK = 4
-WRAP = 176
+WRAP = tuple(2 * math.ceil(128 * math.log(128 * (i + 1) / (1.25 * math.pi)) / math.log(10000)) for i in range(16))
+HEAD_ANGLES = 9
+FIRST_ANGLE_STEP = 1
+WD_ENGINES = "SVSV"
+WR_ENGINES = "VVVV"
+WU_ENGINES = "GGGG"
+WU_EARLY = True
 NI = S // P
 FLOPS = 2 * B * S * D * 3 * QL
 
@@ -34,7 +40,7 @@ def tile_multiheadlatentattention_pa_t_kernel(tc, x_bytes, x_scale, wq_down, wq_
         ctx.enter_context(tc.manual_schedule())
 
         sc4 = keep.tile([P, PACK], F32, name="sc4")
-        nc.sync.dma_start(out=sc4[:], in_=x_scale.rearrange("a b (p t) -> p (a b t)", t=PACK))
+        nc.scalar.dma_start(out=sc4[:], in_=x_scale.rearrange("a b (p t) -> p (a b t)", t=PACK))
         x_view = x_bytes.rearrange("b (i p) k -> p i b k", i=NI)
         x_tiles = {}
 
@@ -52,8 +58,9 @@ def tile_multiheadlatentattention_pa_t_kernel(tc, x_bytes, x_scale, wq_down, wq_
 
         load_x(0, 1)
         wd_raw = load_w(wq_down, "wd_raw")
-        load_x(1, 4)
+        load_x(1, 2)
         wr_raw = load_w(wq_rope, "wr_raw")
+        load_x(2, 4)
         wu_raw = load_w(wq_up, "wu_raw")
         load_x(4, 10)
         load_x(10, 16)
@@ -75,14 +82,14 @@ def tile_multiheadlatentattention_pa_t_kernel(tc, x_bytes, x_scale, wq_down, wq_
         slope = keep.tile([P, NI], F32, name="slope")
         nc.vector.tensor_scalar(slope[:], pos[:], -2 * math.pi, None, op0=ALU.mult)
 
-        turns = keep.tile([P, NI, WRAP], I32, name="turns")
-        frac_all = keep.tile([P, NI, WRAP], F32, name="frac_all")
+        turns = keep.tile([P, NI, WRAP[-1]], I32, name="turns")
+        frac_all = keep.tile([P, NI, WRAP[-1]], F32, name="frac_all")
 
         def count_turns(i):
-            nc.vector.tensor_scalar(turns[:, i, :], freq[:, 0:WRAP], pos[:, i : i + 1], -0.125, op0=ALU.mult, op1=ALU.add)
+            nc.vector.tensor_scalar(turns[:, i, 0 : WRAP[i]], freq[:, 0 : WRAP[i]], pos[:, i : i + 1], -0.125, op0=ALU.mult, op1=ALU.add)
 
         def angle_frac(i):
-            nc.vector.scalar_tensor_tensor(frac_all[:, i, :], freq[:, 0:WRAP], pos[:, i : i + 1], turns[:, i, :], op0=ALU.mult, op1=ALU.subtract)
+            nc.vector.scalar_tensor_tensor(frac_all[:, i, 0 : WRAP[i]], freq[:, 0 : WRAP[i]], pos[:, i : i + 1], turns[:, i, 0 : WRAP[i]], op0=ALU.mult, op1=ALU.subtract)
 
         wd_c = keep.tile([P, 512], U32, name="wd_c", align_bytes=64)
         wd_s = keep.tile([P, 512], U8, name="wd_s", align_bytes=64)
@@ -113,10 +120,10 @@ def tile_multiheadlatentattention_pa_t_kernel(tc, x_bytes, x_scale, wq_down, wq_
                 nc.scalar.copy(widened[i][:, 0:wsplit(i)], x_tiles[i].rearrange("p b k -> p (b k)")[:, 0:wsplit(i)].bitcast(FP8))
 
         def wsplit(i):
-            return 960 if i < 13 else 768
+            return 1024 if i < 12 else 768
 
         def widen_v(i):
-            if i >= 4:
+            if wsplit(i) < B * D:
                 nc.vector.tensor_copy(out=widened[i][:, wsplit(i) : 1024], in_=x_tiles[i].rearrange("p b k -> p (b k)")[:, wsplit(i) : 1024].bitcast(FP8))
 
         def transpose_x(i, bs=(0, 1)):
@@ -185,25 +192,28 @@ def tile_multiheadlatentattention_pa_t_kernel(tc, x_bytes, x_scale, wq_down, wq_
 
         def sines(i):
             ab[i] = work3.tile([P, 2, HALF], F32, name="ab")
-            mag = work.tile([P, WRAP], F32, name="mag")
-            nc.scalar.activation(mag[:], frac_all[:, i, :], ACT.Abs, bias=-0.125, scale=1.0)
-            nc.scalar.activation(ab[i][:, 1, 0:WRAP], frac_all[:, i, :], ACT.Sin, bias=math.pi / 4, scale=-2 * math.pi)
-            nc.scalar.activation(ab[i][:, 1, WRAP:HALF], freq[:, WRAP:HALF], ACT.Sin, bias=math.pi / 4, scale=slope[:, i : i + 1])
-            nc.scalar.activation(ab[i][:, 0, WRAP:HALF], freq[:, WRAP:HALF], ACT.Sin, bias=3 * math.pi / 4, scale=slope[:, i : i + 1])
-            nc.scalar.activation(ab[i][:, 0, 0:WRAP], mag[:], ACT.Sin, bias=math.pi / 2, scale=-2 * math.pi)
+            w = WRAP[i]
+            mag = work.tile([P, WRAP[-1]], F32, name="mag")
+            part = frac_all[:, i, 0:w]
+            nc.scalar.activation(mag[:, 0:w], part, ACT.Abs, bias=-0.125, scale=1.0)
+            nc.scalar.activation(ab[i][:, 1, 0:w], part, ACT.Sin, bias=math.pi / 4, scale=-2 * math.pi)
+            nc.scalar.activation(ab[i][:, 1, w:HALF], freq[:, w:HALF], ACT.Sin, bias=math.pi / 4, scale=slope[:, i : i + 1])
+            nc.scalar.activation(ab[i][:, 0, w:HALF], freq[:, w:HALF], ACT.Sin, bias=3 * math.pi / 4, scale=slope[:, i : i + 1])
+            nc.scalar.activation(ab[i][:, 0, 0:w], mag[:, 0:w], ACT.Sin, bias=math.pi / 2, scale=-2 * math.pi)
 
         def sum_ab(i):
             csum[i] = work.tile([P, HALF], F32, name="csum")
             nc.vector.tensor_tensor(out=csum[i][:], in0=ab[i][:, 0, :], in1=ab[i][:, 1, :], op=ALU.add)
 
-        def rope_products(i):
-            t2[i] = work.tile([P, B, 512], F32, name="t2")
-            for b in range(B):
-                nc.vector.scalar_tensor_tensor(t2[i][:, b, :], rr[i][b][:], math.sqrt(2.0), ab[i][:].rearrange("p f c -> p (f c)"), op0=ALU.mult, op1=ALU.mult)
+        def rope_products(i, b):
+            if b == 0:
+                t2[i] = work.tile([P, B, 512], F32, name="t2")
+            nc.vector.scalar_tensor_tensor(t2[i][:, b, :], rr[i][b][:], math.sqrt(2.0), ab[i][:].rearrange("p f c -> p (f c)"), op0=ALU.mult, op1=ALU.mult)
 
-        def rope_common(i):
-            k1[i] = work.tile([P, B, HALF], F32, name="k1")
-            nc.vector.scalar_tensor_tensor(k1[i][:], rs[i][:], math.sqrt(0.5), csum[i][:].unsqueeze(1).to_broadcast([P, B, HALF]), op0=ALU.mult, op1=ALU.mult)
+        def rope_common(i, b, n):
+            if b == 0:
+                k1[i] = work.tile([P, B, HALF], F32, name="k1")
+            nc.vector.scalar_tensor_tensor(k1[i][:, b : b + n, :], rs[i][:, b : b + n, :], math.sqrt(0.5), csum[i][:].unsqueeze(1).to_broadcast([P, n, HALF]), op0=ALU.mult, op1=ALU.mult)
 
         def copy_proj(i):
             ot[i] = [outs.tile([P, 4, 256], F32, name="ot0"), outs.tile([P, 4, 256], F32, name="ot1")]
@@ -212,27 +222,33 @@ def tile_multiheadlatentattention_pa_t_kernel(tc, x_bytes, x_scale, wq_down, wq_
 
         out_view = out.rearrange("b (i p) h c -> b i p h c", i=NI)
 
-        def rope_sum_and_store(i):
-            if i < NI - 1:
-                gate = work.tile([P, 1], F32, name="gate")
-                nc.gpsimd.tensor_copy(out=gate[:], in_=csum[i + 1][:, 0:1])
-            for b in range(B):
-                last = i == NI - 1 or (i == NI - 2 and b == 1)
-                engine = nc.vector if last else nc.gpsimd
-                for f in range(2) if i == NI - 1 and b == 1 else (slice(0, 2),):
-                    fs = slice(f, f + 1) if isinstance(f, int) else f
-                    n = fs.stop - fs.start
-                    engine.tensor_tensor(
-                        out=ot[i][b][:].rearrange("p (f h) c -> p f h c", f=2)[:, fs, :, 128:256],
-                        in0=k1[i][:, b, :].rearrange("p (h c) -> p h c", h=2).unsqueeze(1).to_broadcast([P, n, 2, 128]),
-                        in1=t2[i][:, b, :].rearrange("p (f h c) -> p f h c", f=2, h=2)[:, fs, :, :],
-                        op=ALU.subtract,
-                    )
-                    nc.sync.dma_start(out=out_view[b, i, :, 2 * fs.start : 2 * fs.stop, :], in_=ot[i][b][:, 2 * fs.start : 2 * fs.stop, :])
+        def rope_sum(i, b, engine, pieces=1):
+            n = 2 // pieces
+            for f in range(0, 2, n):
+                engine.tensor_tensor(
+                    out=ot[i][b][:].rearrange("p (f h) c -> p f h c", f=2)[:, f : f + n, :, 128:256],
+                    in0=k1[i][:, b, :].rearrange("p (h c) -> p h c", h=2).unsqueeze(1).to_broadcast([P, n, 2, 128]),
+                    in1=t2[i][:, b, :].rearrange("p (f h c) -> p f h c", f=2, h=2)[:, f : f + n, :, :],
+                    op=ALU.subtract,
+                )
+                nc.sync.dma_start(out=out_view[b, i, :, 2 * f : 2 * f + 2 * n, :], in_=ot[i][b][:, 2 * f : 2 * f + 2 * n, :])
 
         def at(i, stage):
             if 0 <= i < NI:
                 stage(i)
+
+        def hold_gpsimd(tile):
+            gate = work.tile([P, 1], tile.dtype, name="gate8" if tile.dtype == U8 else "gate32")
+            nc.gpsimd.tensor_copy(out=gate[:], in_=tile[:, 0:1])
+
+        def interleave(engine, grouped, raw, q, src_q):
+            dst = grouped[:, 128 * q : 128 * q + 128, :]
+            src = raw[:, :, 128 * src_q : 128 * src_q + 128]
+            if engine == "G":
+                nc.gpsimd.tensor_scalar(dst, src.rearrange("p j c -> p c j"), 1.0, 0.0, op0=ALU.mult, op1=ALU.add)
+            else:
+                (nc.vector.tensor_copy if engine == "V" else nc.scalar.copy)(
+                    out=dst.rearrange("p (c i) j -> p c j i", i=4), in_=src.rearrange("p j (c i) -> p c j i", i=4))
 
         for i in range(5):
             count_turns(i)
@@ -241,15 +257,16 @@ def tile_multiheadlatentattention_pa_t_kernel(tc, x_bytes, x_scale, wq_down, wq_
         widen(0)
         transpose_x(0, (0,))
         transpose_x(0, (1,))
-        for i in range(5, 8):
+        for i in range(5, HEAD_ANGLES + 1):
             count_turns(i)
         for i in range(5, 7):
             angle_frac(i)
         scale_x(0, (0,))
         scale_x(0, (1,))
+        for i in range(7, HEAD_ANGLES):
+            angle_frac(i)
         for t in range(PACK):
-            interleave = nc.vector.tensor_copy if t % 2 else nc.scalar.copy
-            interleave(
+            (nc.vector.tensor_copy if WD_ENGINES[t] == "V" else nc.scalar.copy)(
                 out=wd_g[:, 128 * t : 128 * t + 128, :],
                 in_=wd_raw[:, :, t : 512 : 4].rearrange("p j m -> p m j"),
             )
@@ -259,45 +276,68 @@ def tile_multiheadlatentattention_pa_t_kernel(tc, x_bytes, x_scale, wq_down, wq_
         quant_x(0)
         quant(wd_c[:], wd_s[:], wd_g[:].rearrange("p n j -> p (n j)"))
         stage1(0)
+        hold_gpsimd(wd_s)
+        if WU_EARLY:
+            interleave("G", wu_g, wu_raw, 0, 0)
+        for q in range(4):
+            if WR_ENGINES[q] == "G":
+                interleave("G", wr_g, wr_raw, q, (q + 2) % 4)
         scale_x(1)
         widen(2)
         transpose_x(2)
         copy_lq(0)
-        for f in range(2):
-            nc.vector.tensor_copy(
-                out=wr_g[:, 256 * f : 256 * f + 256, :].rearrange("p (c i) j -> p c j i", i=4),
-                in_=wr_raw[:, :, 256 - 256 * f : 512 - 256 * f].rearrange("p j (c i) -> p c j i", i=4),
-            )
+        for q in range(4):
+            if WR_ENGINES[q] != "G":
+                interleave(WR_ENGINES[q], wr_g, wr_raw, q, (q + 2) % 4)
         quant_x(1)
         stage1(1)
         quant_lq(0)
         quant(wr_c[:], wr_s[:], wr_g[:].rearrange("p n j -> p (n j)"))
         sum_ab(0)
-        for f in range(2):
-            (nc.vector.tensor_copy if f else nc.scalar.copy)(
-                out=wu_g[:, 256 * f : 256 * f + 256, :].rearrange("p (c i) j -> p c j i", i=4),
-                in_=wu_raw[:, :, 256 * f : 256 * f + 256].rearrange("p j (c i) -> p c j i", i=4),
-            )
+        hold_gpsimd(csum[0])
+        for q in range(4):
+            if WU_ENGINES[q] != "S" and (q > 0 or not WU_EARLY):
+                interleave(WU_ENGINES[q], wu_g, wu_raw, q, q)
         widen(3)
         sines(1)
-        for k in range(0, NI + 1):
+        for k in range(0, NI):
             at(k, rope_mm)
             at(k + 2, scale_x)
             at(k + 1, copy_lq)
-            at(k, rope_products)
-            at(k, rope_common)
-            if k == 0:
-                quant(wu_c[:], wu_s[:], wu_g[:].rearrange("p n j -> p (n j)"))
-            at(k, proj_mm)
+            if k == NI - 1:
+                rope_sum(k - 1, 1, nc.vector)
+            for b in range(B):
+                rope_products(k, b)
+                if k == NI - 1:
+                    rope_common(k, b, 1)
+            if k < NI - 1:
+                rope_common(k, 0, B)
             at(k + 3, transpose_x)
-            at(k, copy_proj)
-            at(k - 1, rope_sum_and_store)
+            if k != 0:
+                at(k, proj_mm)
+            if 1 <= k < NI:
+                hold_gpsimd(csum[k])
+                for b in range(B if k < NI - 1 else 1):
+                    rope_sum(k - 1, b, nc.gpsimd)
             at(k + 4, widen)
             at(k + 2, sines)
+            if k != 0:
+                at(k, copy_proj)
             at(k + 2, quant_x)
             at(k + 2, stage1)
             at(k + 1, quant_lq)
-            at(k + 7, angle_frac)
+            if k == 0:
+                for q in range(4):
+                    if WU_ENGINES[q] == "S":
+                        interleave("S", wu_g, wu_raw, q, q)
+                quant(wu_c[:], wu_s[:], wu_g[:].rearrange("p n j -> p (n j)"))
+                proj_mm(0)
+                copy_proj(0)
+            if k >= FIRST_ANGLE_STEP:
+                at(k - FIRST_ANGLE_STEP + HEAD_ANGLES, angle_frac)
             at(k + 4, widen_v)
-            at(k + 8, count_turns)
+            if k >= FIRST_ANGLE_STEP:
+                at(k - FIRST_ANGLE_STEP + HEAD_ANGLES + 1, count_turns)
             at(k + 1, sum_ab)
+        rope_sum(NI - 1, 0, nc.vector)
+        rope_sum(NI - 1, 1, nc.vector, pieces=2)

@@ -10,9 +10,11 @@ P = 128
 PACK = 4
 WRAP = tuple(2 * math.ceil(128 * math.log(128 * (i + 1) / (1.25 * math.pi)) / math.log(10000)) for i in range(16))
 HEAD_ANGLES = 9
-FIRST_ANGLE_STEP = 1
+FIRST_ANGLE_STEP = 0
+WIDE = (1024, 1024, 1024, 1024, 1024, 1024, 1024, 1024, 896, 1024, 896, 768, 768, 768, 768, 768)
+S_ORDER = "DWTF"
 WD_ENGINES = "SVSV"
-WR_ENGINES = "VVVV"
+WR_ENGINES = "VVVS"
 WU_ENGINES = "GGGG"
 WU_EARLY = True
 NI = S // P
@@ -35,6 +37,7 @@ def tile_multiheadlatentattention_pa_t_kernel(tc, x_bytes, x_scale, wq_down, wq_
         keep = ctx.enter_context(tc.tile_pool(name="keep", bufs=1))
         work = ctx.enter_context(tc.tile_pool(name="work", bufs=2))
         work3 = ctx.enter_context(tc.tile_pool(name="work3", bufs=3))
+        deep = ctx.enter_context(tc.tile_pool(name="deep", bufs=16))
         outs = ctx.enter_context(tc.tile_pool(name="outs", bufs=3))
         ps1 = ctx.enter_context(tc.psum_pool(name="ps1", bufs=1))
         ctx.enter_context(tc.manual_schedule())
@@ -114,13 +117,11 @@ def tile_multiheadlatentattention_pa_t_kernel(tc, x_bytes, x_scale, wq_down, wq_
             if i == 0:
                 nc.scalar.copy(widened[i][:, 0:D], x_tiles[i][:, 0, :].bitcast(FP8))
                 nc.vector.tensor_copy(out=widened[i][:, D : 2 * D], in_=x_tiles[i][:, 1, :].bitcast(FP8))
-            elif i < 4:
-                nc.scalar.copy(widened[i][:], x_tiles[i].rearrange("p b k -> p (b k)").bitcast(FP8))
             else:
                 nc.scalar.copy(widened[i][:, 0:wsplit(i)], x_tiles[i].rearrange("p b k -> p (b k)")[:, 0:wsplit(i)].bitcast(FP8))
 
         def wsplit(i):
-            return 1024 if i < 12 else 768
+            return WIDE[i]
 
         def widen_v(i):
             if wsplit(i) < B * D:
@@ -207,31 +208,30 @@ def tile_multiheadlatentattention_pa_t_kernel(tc, x_bytes, x_scale, wq_down, wq_
 
         def rope_products(i, b):
             if b == 0:
-                t2[i] = work.tile([P, B, 512], F32, name="t2")
+                t2[i] = deep.tile([P, B, 512], F32, name="t2")
             nc.vector.scalar_tensor_tensor(t2[i][:, b, :], rr[i][b][:], math.sqrt(2.0), ab[i][:].rearrange("p f c -> p (f c)"), op0=ALU.mult, op1=ALU.mult)
 
         def rope_common(i, b, n):
             if b == 0:
-                k1[i] = work.tile([P, B, HALF], F32, name="k1")
+                k1[i] = deep.tile([P, B, HALF], F32, name="k1")
             nc.vector.scalar_tensor_tensor(k1[i][:, b : b + n, :], rs[i][:, b : b + n, :], math.sqrt(0.5), csum[i][:].unsqueeze(1).to_broadcast([P, n, HALF]), op0=ALU.mult, op1=ALU.mult)
 
         def copy_proj(i):
-            ot[i] = [outs.tile([P, 4, 256], F32, name="ot0"), outs.tile([P, 4, 256], F32, name="ot1")]
+            ot[i] = outs.tile([P, B, 4, 256], F32, name="ot")
             for b in range(B):
-                nc.scalar.copy(ot[i][b][:, :, 0:128], qp[i][b][:].rearrange("p (h c) -> p h c", h=4))
+                nc.scalar.copy(ot[i][:, b, :, 0:128], qp[i][b][:].rearrange("p (h c) -> p h c", h=4))
 
         out_view = out.rearrange("b (i p) h c -> b i p h c", i=NI)
 
-        def rope_sum(i, b, engine, pieces=1):
-            n = 2 // pieces
-            for f in range(0, 2, n):
-                engine.tensor_tensor(
-                    out=ot[i][b][:].rearrange("p (f h) c -> p f h c", f=2)[:, f : f + n, :, 128:256],
-                    in0=k1[i][:, b, :].rearrange("p (h c) -> p h c", h=2).unsqueeze(1).to_broadcast([P, n, 2, 128]),
-                    in1=t2[i][:, b, :].rearrange("p (f h c) -> p f h c", f=2, h=2)[:, f : f + n, :, :],
-                    op=ALU.subtract,
-                )
-                nc.sync.dma_start(out=out_view[b, i, :, 2 * f : 2 * f + 2 * n, :], in_=ot[i][b][:, 2 * f : 2 * f + 2 * n, :])
+        def rope_sum(i, b, n, engine, f=0, m=2):
+            engine.tensor_tensor(
+                out=ot[i][:].rearrange("p b (f h) c -> p b f h c", f=2)[:, b : b + n, f : f + m, :, 128:256],
+                in0=k1[i][:, b : b + n, :].rearrange("p b (h c) -> p b h c", h=2).unsqueeze(2).to_broadcast([P, n, m, 2, 128]),
+                in1=t2[i][:, b : b + n, :].rearrange("p b (f h c) -> p b f h c", f=2, h=2)[:, :, f : f + m, :, :],
+                op=ALU.subtract,
+            )
+            for bb in range(b, b + n):
+                nc.sync.dma_start(out=out_view[bb, i, :, 2 * f : 2 * f + 2 * m, :], in_=ot[i][:, bb, 2 * f : 2 * f + 2 * m, :])
 
         def at(i, stage):
             if 0 <= i < NI:
@@ -250,15 +250,27 @@ def tile_multiheadlatentattention_pa_t_kernel(tc, x_bytes, x_scale, wq_down, wq_
                 (nc.vector.tensor_copy if engine == "V" else nc.scalar.copy)(
                     out=dst.rearrange("p (c i) j -> p c j i", i=4), in_=src.rearrange("p j (c i) -> p c j i", i=4))
 
+        def s_turn(k, n):
+            what = S_ORDER[n]
+            if what == "D":
+                at(k + 1, copy_lq)
+            elif what == "W":
+                at(k + 4, widen)
+            elif what == "T":
+                at(k + 2, sines)
+            elif k != 0:
+                at(k, copy_proj)
+
         for i in range(5):
             count_turns(i)
         for i in range(5):
             angle_frac(i)
+        for i in range(5, HEAD_ANGLES + 1):
+            count_turns(i)
         widen(0)
         transpose_x(0, (0,))
         transpose_x(0, (1,))
-        for i in range(5, HEAD_ANGLES + 1):
-            count_turns(i)
+        sines(0)
         for i in range(5, 7):
             angle_frac(i)
         scale_x(0, (0,))
@@ -272,7 +284,6 @@ def tile_multiheadlatentattention_pa_t_kernel(tc, x_bytes, x_scale, wq_down, wq_
             )
         widen(1)
         transpose_x(1)
-        sines(0)
         quant_x(0)
         quant(wd_c[:], wd_s[:], wd_g[:].rearrange("p n j -> p (n j)"))
         stage1(0)
@@ -303,9 +314,11 @@ def tile_multiheadlatentattention_pa_t_kernel(tc, x_bytes, x_scale, wq_down, wq_
         for k in range(0, NI):
             at(k, rope_mm)
             at(k + 2, scale_x)
-            at(k + 1, copy_lq)
+            s_turn(k, 0)
             if k == NI - 1:
-                rope_sum(k - 1, 1, nc.vector)
+                rope_sum(k - 1, 1, 1, nc.vector)
+            if k == NI - 2:
+                rope_sum(k - 1, 0, 1, nc.vector)
             for b in range(B):
                 rope_products(k, b)
                 if k == NI - 1:
@@ -317,12 +330,17 @@ def tile_multiheadlatentattention_pa_t_kernel(tc, x_bytes, x_scale, wq_down, wq_
                 at(k, proj_mm)
             if 1 <= k < NI:
                 hold_gpsimd(csum[k])
-                for b in range(B if k < NI - 1 else 1):
-                    rope_sum(k - 1, b, nc.gpsimd)
-            at(k + 4, widen)
-            at(k + 2, sines)
-            if k != 0:
-                at(k, copy_proj)
+                if k - 1 < 12:
+                    rope_sum(k - 1, 0, B, nc.gpsimd)
+                elif k - 1 == 12:
+                    rope_sum(k - 1, 0, 1, nc.gpsimd)
+                    rope_sum(k - 1, 1, 1, nc.gpsimd)
+                elif k - 1 == 13:
+                    rope_sum(k - 1, 1, 1, nc.gpsimd)
+                else:
+                    rope_sum(k - 1, 0, 1, nc.gpsimd)
+            for n in (1, 2, 3):
+                s_turn(k, n)
             at(k + 2, quant_x)
             at(k + 2, stage1)
             at(k + 1, quant_lq)
@@ -339,5 +357,6 @@ def tile_multiheadlatentattention_pa_t_kernel(tc, x_bytes, x_scale, wq_down, wq_
             if k >= FIRST_ANGLE_STEP:
                 at(k - FIRST_ANGLE_STEP + HEAD_ANGLES + 1, count_turns)
             at(k + 1, sum_ab)
-        rope_sum(NI - 1, 0, nc.vector)
-        rope_sum(NI - 1, 1, nc.vector, pieces=2)
+        rope_sum(NI - 1, 0, 1, nc.vector)
+        for f in range(2):
+            rope_sum(NI - 1, 1, 1, nc.vector, f, 1)

import math
from contextlib import ExitStack

import concourse.mybir as mybir
from concourse.masks import make_identity

B, S, D, QL = 2, 2048, 512, 512
HALF = 256
P = 128
PACK = 4
WRAP = tuple(2 * math.ceil(128 * math.log(128 * (i + 1) / (1.25 * math.pi)) / math.log(10000)) for i in range(16))
HEAD_ANGLES = 9
FIRST_ANGLE_STEP = 0
WIDE = (1024, 1024, 1024, 1024, 1024, 1024, 1024, 1024, 896, 1024, 896, 768, 768, 768, 768, 768)
S_ORDER = "DWTF"
WD_ENGINES = "SVSV"
WR_ENGINES = "VVVS"
WU_ENGINES = "GGGG"
WU_EARLY = True
NI = S // P
FLOPS = 2 * B * S * D * 3 * QL

F32 = mybir.dt.float32
BF16 = mybir.dt.bfloat16
I32 = mybir.dt.int32
U32 = mybir.dt.uint32
U8 = mybir.dt.uint8
FP8 = mybir.dt.float8_e4m3fn
FP8X4 = mybir.dt.float8_e4m3fn_x4
ALU = mybir.AluOpType
ACT = mybir.ActivationFunctionType


def tile_multiheadlatentattention_pa_t_kernel(tc, x_bytes, x_scale, wq_down, wq_up, wq_rope, out):
    nc = tc.nc
    with ExitStack() as ctx:
        keep = ctx.enter_context(tc.tile_pool(name="keep", bufs=1))
        work = ctx.enter_context(tc.tile_pool(name="work", bufs=2))
        work3 = ctx.enter_context(tc.tile_pool(name="work3", bufs=3))
        deep = ctx.enter_context(tc.tile_pool(name="deep", bufs=16))
        outs = ctx.enter_context(tc.tile_pool(name="outs", bufs=3))
        ps1 = ctx.enter_context(tc.psum_pool(name="ps1", bufs=1))
        ctx.enter_context(tc.manual_schedule())

        sc4 = keep.tile([P, PACK], F32, name="sc4")
        nc.scalar.dma_start(out=sc4[:], in_=x_scale.rearrange("a b (p t) -> p (a b t)", t=PACK))
        x_view = x_bytes.rearrange("b (i p) k -> p i b k", i=NI)
        x_tiles = {}

        def load_x(lo, hi):
            t = keep.tile([P, hi - lo, B, D], U8, name="xb%d" % lo)
            for b in range(B):
                nc.sync.dma_start(out=t[:, :, b, :], in_=x_view[:, lo:hi, b, :])
            for i in range(lo, hi):
                x_tiles[i] = t[:, i - lo, :, :]

        def load_w(w, name):
            t = keep.tile([P, PACK, 512], BF16, name=name)
            nc.sync.dma_start(out=t[:], in_=w.rearrange("(p j) c -> p j c", j=PACK))
            return t

        load_x(0, 1)
        wd_raw = load_w(wq_down, "wd_raw")
        load_x(1, 2)
        wr_raw = load_w(wq_rope, "wr_raw")
        load_x(2, 4)
        wu_raw = load_w(wq_up, "wu_raw")
        load_x(4, 10)
        load_x(10, 16)

        pos = keep.tile([P, NI], F32, name="pos")
        nc.gpsimd.iota(pos[:], pattern=[[P, NI]], base=0, channel_multiplier=1, allow_small_or_imprecise_dtypes=True)
        ident = keep.tile([P, P], F32, name="ident")
        make_identity(nc, ident[:])
        ones = keep.tile([P, 1], F32, name="ones")
        nc.vector.memset(ones[:], 1.0)
        dummy = keep.tile([P, 1], F32, name="dummy")
        nc.scalar.activation(dummy[:], ones[:], ACT.Sin)
        freq = keep.tile([P, HALF], F32, name="freq")
        for j in range(8):
            nc.vector.tensor_scalar(freq[:, j : j + 1], ones[:], 10000.0 ** (-j / 256.0) / (2.0 * math.pi), None, op0=ALU.mult)
        for width in (8, 64):
            for m in range(1, min(8, HALF // width)):
                nc.vector.tensor_scalar(freq[:, m * width : (m + 1) * width], freq[:, 0:width], 10000.0 ** (-m * width / 256.0), None, op0=ALU.mult)
        slope = keep.tile([P, NI], F32, name="slope")
        nc.vector.tensor_scalar(slope[:], pos[:], -2 * math.pi, None, op0=ALU.mult)

        turns = keep.tile([P, NI, WRAP[-1]], I32, name="turns")
        frac_all = keep.tile([P, NI, WRAP[-1]], F32, name="frac_all")

        def count_turns(i):
            nc.vector.tensor_scalar(turns[:, i, 0 : WRAP[i]], freq[:, 0 : WRAP[i]], pos[:, i : i + 1], -0.125, op0=ALU.mult, op1=ALU.add)

        def angle_frac(i):
            nc.vector.scalar_tensor_tensor(frac_all[:, i, 0 : WRAP[i]], freq[:, 0 : WRAP[i]], pos[:, i : i + 1], turns[:, i, 0 : WRAP[i]], op0=ALU.mult, op1=ALU.subtract)

        wd_c = keep.tile([P, 512], U32, name="wd_c", align_bytes=64)
        wd_s = keep.tile([P, 512], U8, name="wd_s", align_bytes=64)
        wr_c = keep.tile([P, 512], U32, name="wr_c", align_bytes=64)
        wr_s = keep.tile([P, 512], U8, name="wr_s", align_bytes=64)
        wu_c = keep.tile([P, 512], U32, name="wu_c", align_bytes=64)
        wu_s = keep.tile([P, 512], U8, name="wu_s", align_bytes=64)
        wd_g = keep.tile([P, 512, PACK], BF16, name="wd_g", align_bytes=64)
        wr_g = keep.tile([P, 512, PACK], BF16, name="wr_g", align_bytes=64)
        wu_g = keep.tile([P, 512, PACK], BF16, name="wu_g", align_bytes=64)

        def quant(codes, scales, src):
            nc.vector.quantize_mx(out=codes.bitcast(FP8X4), scales=scales, in_=src)

        def mm(o, lc, ls, rc, rs_, start=True, stop=True):
            nc.tensor.matmul_mx(out=o, lhsT=lc.bitcast(FP8X4), lhsT_scale=ls, rhs=rc.bitcast(FP8X4), rhs_scale=rs_, start=start, stop=stop)

        widened, xt, xg, xq, lq, lb, lqq, rr, rs, qp, ab, csum, t2, k1, ot = ({} for _ in range(15))

        def widen(i):
            widened[i] = work3.tile([P, B * D], BF16, name="widened")
            if i == 0:
                nc.scalar.copy(widened[i][:, 0:D], x_tiles[i][:, 0, :].bitcast(FP8))
                nc.vector.tensor_copy(out=widened[i][:, D : 2 * D], in_=x_tiles[i][:, 1, :].bitcast(FP8))
            else:
                nc.scalar.copy(widened[i][:, 0:wsplit(i)], x_tiles[i].rearrange("p b k -> p (b k)")[:, 0:wsplit(i)].bitcast(FP8))

        def wsplit(i):
            return WIDE[i]

        def widen_v(i):
            if wsplit(i) < B * D:
                nc.vector.tensor_copy(out=widened[i][:, wsplit(i) : 1024], in_=x_tiles[i].rearrange("p b k -> p (b k)")[:, wsplit(i) : 1024].bitcast(FP8))

        def transpose_x(i, bs=(0, 1)):
            if bs[0] == 0:
                xt[i] = ps1.tile([P, 2, 256], F32, name="xt")
            words = widened[i][:].bitcast(F32)
            for b in bs:
                for u in range(2):
                    nc.tensor.transpose(xt[i][:, u, 128 * b : 128 * b + 128], words[:, 256 * b + u : 256 * (b + 1) : 2], ident[:])

        def scale_x(i, bs=(0, 1)):
            if bs[0] == 0:
                xg[i] = work.tile([P, 256, PACK], BF16, name="xg", align_bytes=64)
            lo, n = 128 * bs[0], 128 * len(bs)
            nc.vector.tensor_tensor(
                out=xg[i][:, lo : lo + n, :].rearrange("p r (u e) -> p r u e", u=2),
                in0=xt[i][:].rearrange("p u r -> p (u r)").bitcast(BF16).rearrange("p (u r e) -> p r u e", u=2, e=2)[:, lo : lo + n, :, :],
                in1=sc4[:].rearrange("p (u e) -> p u e", u=2).unsqueeze(1).to_broadcast([P, n, 2, 2]),
                op=ALU.mult,
            )

        def quant_x(i):
            c = work3.tile([P, 256], U32, name="xq_c", align_bytes=64)
            s = work3.tile([P, 256], U8, name="xq_s", align_bytes=64)
            quant(c[:], s[:], xg[i][:].rearrange("p r j -> p (r j)"))
            xq[i] = (c, s)

        def stage1(i):
            c, s = xq[i]
            lq[i] = [ps1.tile([P, PACK, 128], F32, name="lq0"), ps1.tile([P, PACK, 128], F32, name="lq1")]
            for b in range(B):
                cols = slice(128 * b, 128 * b + 128)
                for t in range(PACK):
                    wcols = slice(128 * t, 128 * t + 128)
                    mm(lq[i][b][:, t, :], wd_c[:, wcols], wd_s[:, wcols], c[:, cols], s[:, cols])

        def copy_lq(i):
            lb[i] = work.tile([P, B, 128, PACK], BF16, name="lb", align_bytes=64)
            for b in range(B):
                nc.scalar.copy(lb[i][:, b, :, :], lq[i][b][:].rearrange("p t r -> p r t"))

        def quant_lq(i):
            c = work3.tile([P, 256], U32, name="lq_c", align_bytes=64)
            s = work3.tile([P, 256], U8, name="lq_s", align_bytes=64)
            quant(c[:], s[:], lb[i][:].rearrange("p b r j -> p (b r j)"))
            lqq[i] = (c, s)

        def rope_mm(i):
            c, s = lqq[i]
            rr[i] = [ps1.tile([P, 512], F32, name="rr0"), ps1.tile([P, 512], F32, name="rr1")]
            rs[i] = ps1.tile([P, B, HALF], F32, name="rs")
            for b in range(B):
                cols = slice(128 * b, 128 * b + 128)
                mm(rr[i][b][:], c[:, cols], s[:, cols], wr_c[:], wr_s[:])
            for b in range(B):
                cols = slice(128 * b, 128 * b + 128)
                mm(rs[i][:, b, :], c[:, cols], s[:, cols], wr_c[:, 0:HALF], wr_s[:, 0:HALF], start=True, stop=False)
                mm(rs[i][:, b, :], c[:, cols], s[:, cols], wr_c[:, HALF:512], wr_s[:, HALF:512], start=False, stop=True)

        def proj_mm(i):
            c, s = lqq[i]
            qp[i] = [ps1.tile([P, 512], F32, name="qp0"), ps1.tile([P, 512], F32, name="qp1")]
            for b in range(B):
                cols = slice(128 * b, 128 * b + 128)
                mm(qp[i][b][:], c[:, cols], s[:, cols], wu_c[:], wu_s[:])

        def sines(i):
            ab[i] = work3.tile([P, 2, HALF], F32, name="ab")
            w = WRAP[i]
            mag = work.tile([P, WRAP[-1]], F32, name="mag")
            part = frac_all[:, i, 0:w]
            nc.scalar.activation(mag[:, 0:w], part, ACT.Abs, bias=-0.125, scale=1.0)
            nc.scalar.activation(ab[i][:, 1, 0:w], part, ACT.Sin, bias=math.pi / 4, scale=-2 * math.pi)
            nc.scalar.activation(ab[i][:, 1, w:HALF], freq[:, w:HALF], ACT.Sin, bias=math.pi / 4, scale=slope[:, i : i + 1])
            nc.scalar.activation(ab[i][:, 0, w:HALF], freq[:, w:HALF], ACT.Sin, bias=3 * math.pi / 4, scale=slope[:, i : i + 1])
            nc.scalar.activation(ab[i][:, 0, 0:w], mag[:, 0:w], ACT.Sin, bias=math.pi / 2, scale=-2 * math.pi)

        def sum_ab(i):
            csum[i] = work.tile([P, HALF], F32, name="csum")
            nc.vector.tensor_tensor(out=csum[i][:], in0=ab[i][:, 0, :], in1=ab[i][:, 1, :], op=ALU.add)

        def rope_products(i, b):
            if b == 0:
                t2[i] = deep.tile([P, B, 512], F32, name="t2")
            nc.vector.scalar_tensor_tensor(t2[i][:, b, :], rr[i][b][:], math.sqrt(2.0), ab[i][:].rearrange("p f c -> p (f c)"), op0=ALU.mult, op1=ALU.mult)

        def rope_common(i, b, n):
            if b == 0:
                k1[i] = deep.tile([P, B, HALF], F32, name="k1")
            nc.vector.scalar_tensor_tensor(k1[i][:, b : b + n, :], rs[i][:, b : b + n, :], math.sqrt(0.5), csum[i][:].unsqueeze(1).to_broadcast([P, n, HALF]), op0=ALU.mult, op1=ALU.mult)

        def copy_proj(i):
            ot[i] = outs.tile([P, B, 4, 256], F32, name="ot")
            for b in range(B):
                nc.scalar.copy(ot[i][:, b, :, 0:128], qp[i][b][:].rearrange("p (h c) -> p h c", h=4))

        out_view = out.rearrange("b (i p) h c -> b i p h c", i=NI)

        def rope_sum(i, b, n, engine, f=0, m=2):
            engine.tensor_tensor(
                out=ot[i][:].rearrange("p b (f h) c -> p b f h c", f=2)[:, b : b + n, f : f + m, :, 128:256],
                in0=k1[i][:, b : b + n, :].rearrange("p b (h c) -> p b h c", h=2).unsqueeze(2).to_broadcast([P, n, m, 2, 128]),
                in1=t2[i][:, b : b + n, :].rearrange("p b (f h c) -> p b f h c", f=2, h=2)[:, :, f : f + m, :, :],
                op=ALU.subtract,
            )
            for bb in range(b, b + n):
                nc.sync.dma_start(out=out_view[bb, i, :, 2 * f : 2 * f + 2 * m, :], in_=ot[i][:, bb, 2 * f : 2 * f + 2 * m, :])

        def at(i, stage):
            if 0 <= i < NI:
                stage(i)

        def hold_gpsimd(tile):
            gate = work.tile([P, 1], tile.dtype, name="gate8" if tile.dtype == U8 else "gate32")
            nc.gpsimd.tensor_copy(out=gate[:], in_=tile[:, 0:1])

        def interleave(engine, grouped, raw, q, src_q):
            dst = grouped[:, 128 * q : 128 * q + 128, :]
            src = raw[:, :, 128 * src_q : 128 * src_q + 128]
            if engine == "G":
                nc.gpsimd.tensor_scalar(dst, src.rearrange("p j c -> p c j"), 1.0, 0.0, op0=ALU.mult, op1=ALU.add)
            else:
                (nc.vector.tensor_copy if engine == "V" else nc.scalar.copy)(
                    out=dst.rearrange("p (c i) j -> p c j i", i=4), in_=src.rearrange("p j (c i) -> p c j i", i=4))

        def s_turn(k, n):
            what = S_ORDER[n]
            if what == "D":
                at(k + 1, copy_lq)
            elif what == "W":
                at(k + 4, widen)
            elif what == "T":
                at(k + 2, sines)
            elif k != 0:
                at(k, copy_proj)

        for i in range(5):
            count_turns(i)
        for i in range(5):
            angle_frac(i)
        for i in range(5, HEAD_ANGLES + 1):
            count_turns(i)
        widen(0)
        transpose_x(0, (0,))
        transpose_x(0, (1,))
        sines(0)
        for i in range(5, 7):
            angle_frac(i)
        scale_x(0, (0,))
        scale_x(0, (1,))
        for i in range(7, HEAD_ANGLES):
            angle_frac(i)
        for t in range(PACK):
            (nc.vector.tensor_copy if WD_ENGINES[t] == "V" else nc.scalar.copy)(
                out=wd_g[:, 128 * t : 128 * t + 128, :],
                in_=wd_raw[:, :, t : 512 : 4].rearrange("p j m -> p m j"),
            )
        widen(1)
        transpose_x(1)
        quant_x(0)
        quant(wd_c[:], wd_s[:], wd_g[:].rearrange("p n j -> p (n j)"))
        stage1(0)
        hold_gpsimd(wd_s)
        if WU_EARLY:
            interleave("G", wu_g, wu_raw, 0, 0)
        for q in range(4):
            if WR_ENGINES[q] == "G":
                interleave("G", wr_g, wr_raw, q, (q + 2) % 4)
        scale_x(1)
        widen(2)
        transpose_x(2)
        copy_lq(0)
        for q in range(4):
            if WR_ENGINES[q] != "G":
                interleave(WR_ENGINES[q], wr_g, wr_raw, q, (q + 2) % 4)
        quant_x(1)
        stage1(1)
        quant_lq(0)
        quant(wr_c[:], wr_s[:], wr_g[:].rearrange("p n j -> p (n j)"))
        sum_ab(0)
        hold_gpsimd(csum[0])
        for q in range(4):
            if WU_ENGINES[q] != "S" and (q > 0 or not WU_EARLY):
                interleave(WU_ENGINES[q], wu_g, wu_raw, q, q)
        widen(3)
        sines(1)
        for k in range(0, NI):
            at(k, rope_mm)
            at(k + 2, scale_x)
            s_turn(k, 0)
            if k == NI - 1:
                rope_sum(k - 1, 1, 1, nc.vector)
            if k == NI - 2:
                rope_sum(k - 1, 0, 1, nc.vector)
            for b in range(B):
                rope_products(k, b)
                if k == NI - 1:
                    rope_common(k, b, 1)
            if k < NI - 1:
                rope_common(k, 0, B)
            at(k + 3, transpose_x)
            if k != 0:
                at(k, proj_mm)
            if 1 <= k < NI:
                hold_gpsimd(csum[k])
                if k - 1 < 12:
                    rope_sum(k - 1, 0, B, nc.gpsimd)
                elif k - 1 == 12:
                    rope_sum(k - 1, 0, 1, nc.gpsimd)
                    rope_sum(k - 1, 1, 1, nc.gpsimd)
                elif k - 1 == 13:
                    rope_sum(k - 1, 1, 1, nc.gpsimd)
                else:
                    rope_sum(k - 1, 0, 1, nc.gpsimd)
            for n in (1, 2, 3):
                s_turn(k, n)
            at(k + 2, quant_x)
            at(k + 2, stage1)
            at(k + 1, quant_lq)
            if k == 0:
                for q in range(4):
                    if WU_ENGINES[q] == "S":
                        interleave("S", wu_g, wu_raw, q, q)
                quant(wu_c[:], wu_s[:], wu_g[:].rearrange("p n j -> p (n j)"))
                proj_mm(0)
                copy_proj(0)
            if k >= FIRST_ANGLE_STEP:
                at(k - FIRST_ANGLE_STEP + HEAD_ANGLES, angle_frac)
            at(k + 4, widen_v)
            if k >= FIRST_ANGLE_STEP:
                at(k - FIRST_ANGLE_STEP + HEAD_ANGLES + 1, count_turns)
            at(k + 1, sum_ab)
        rope_sum(NI - 1, 0, 1, nc.vector)
        for f in range(2):
            rope_sum(NI - 1, 1, 1, nc.vector, f, 1)
